import numpy as np
import ml_dtypes


def mxq(x, axis, fmt="e4m3"):
    dtype, down = {"e4m3": (ml_dtypes.float8_e4m3fn, 7), "e5m2": (ml_dtypes.float8_e5m2, 14)}[fmt]
    v = np.moveaxis(np.asarray(x, np.float32).astype(ml_dtypes.bfloat16).astype(np.float64), axis, -1)
    blocks = v.reshape(v.shape[:-1] + (-1, 32))
    amax = np.abs(blocks).max(-1, keepdims=True)
    byte = np.maximum(np.where(amax > 0, np.frexp(amax)[1] - 1 + 127, 0) - down, 1)
    scale = np.exp2(byte - 127.0)
    codes = (blocks / scale).astype(np.float32).astype(dtype).astype(np.float64)
    return np.moveaxis((codes * scale).reshape(v.shape), -1, axis)


WIDE = False


def mx_kscale(k):
    if not WIDE:
        return np.ones(k)
    levels = np.array([10, -10, 5, -5, 0])
    if k % 512:
        return np.exp2(np.random.permutation(np.resize(levels, k // 32))).repeat(32)
    a = np.empty((k // 512, 16))
    for p in range(k // 512):
        a[p, :8] = np.random.permutation(np.resize(levels, 8))
        for g in range(8):
            far = levels[np.abs(levels - a[p, g]) >= 10]
            a[p, g + 8] = far[np.random.randint(len(far))]
    return np.exp2(a.ravel()).repeat(32)


BF16 = ml_dtypes.bfloat16


def bf(x):
    return np.asarray(x, np.float32).astype(BF16)


def f64(x):
    return np.asarray(x).astype(np.float64)


B, S, DIM, H, NKV, HD, GS = 1, 512, 2048, 16, 4, 128, 128
QS = H * HD
KVS = NKV * HD
HALF = HD // 2
ROPE_BASE = 10000.0
RMS_EPS = 1.1920929e-07


def rms_norm(v):
    return v / np.sqrt(np.mean(v * v, axis=-1, keepdims=True) + RMS_EPS)


def rope_cos_sin():
    inv_freq = 1.0 / ROPE_BASE ** (np.arange(0, HD, 2) / HD)
    freqs = np.outer(np.arange(S), inv_freq)
    return np.cos(freqs)[None, :, None, :], np.sin(freqs)[None, :, None, :]


def apply_rotary_emb(u, cos, sin):
    u1, u2 = u[..., :HALF], u[..., HALF:]
    return np.concatenate((u1 * cos + u2 * sin, u1 * -sin + u2 * cos), axis=-1)


def draw0():
    s = mx_kscale(DIM)
    return {"x": bf(np.random.standard_normal((B, S, DIM)) * s),
            "w_qkv_tern": bf(np.random.standard_normal((QS + 2 * KVS, DIM)) * 0.66 / np.sqrt(DIM) / s[None, :]),
            "q_gain": bf(1.0 + 0.1 * np.random.standard_normal(H))}


def core(x, w_qkv_tern, q_gain):
    qkv = mxq(f64(x), 2, "e4m3") @ mxq(f64(w_qkv_tern), 1, "e4m3").T
    q = qkv[..., :QS].reshape(B, S, H, HD)
    k = qkv[..., QS:QS + KVS].reshape(B, S, NKV, HD)
    v = qkv[..., QS + KVS:].reshape(B, S, NKV, HD)
    q, k = rms_norm(q), rms_norm(k)
    cos, sin = rope_cos_sin()
    q = apply_rotary_emb(q, cos, sin)
    k = apply_rotary_emb(k, cos, sin)
    q = q * f64(q_gain)[None, None, :, None]
    return q, k, v


def e4m3fn_bytes(y):
    return np.clip(np.asarray(y, np.float64), -448.0, 448.0).astype(np.float32).astype(ml_dtypes.float8_e4m3fn).view(np.uint8)


def e4m3fn_values(b):
    return np.asarray(b, np.uint8).view(ml_dtypes.float8_e4m3fn).astype(np.float64)


def setup_inputs():
    d = draw0()
    x0 = np.asarray(d['w_qkv_tern']).astype(np.float64)
    s = (np.max(np.abs(x0), axis=(0,), keepdims=True) / 448.0).astype(np.float32)
    out = {}
    for k, v in d.items():
        if k == 'w_qkv_tern':
            out['w_qkv_tern_bytes'] = e4m3fn_bytes(x0 / s.astype(np.float64))
            out['w_qkv_tern_scale'] = s
        else:
            out[k] = v
    return out


def reference(x, w_qkv_tern_bytes, w_qkv_tern_scale, q_gain):
    return core(x, e4m3fn_values(w_qkv_tern_bytes) * w_qkv_tern_scale.astype(np.float64), q_gain)

@@ -1,0 +1,378 @@
+from contextlib import ExitStack
+import math
+
+import concourse.mybir as mybir
+from concourse.masks import make_identity
+
+FLOPS = 2 * 512 * 3072 * 2048
+
+F32 = mybir.dt.float32
+BF16 = mybir.dt.bfloat16
+I32 = mybir.dt.int32
+U32 = mybir.dt.uint32
+U8 = mybir.dt.uint8
+FP8 = mybir.dt.float8_e4m3fn
+FP8X4 = mybir.dt.float8_e4m3fn_x4
+ALU = mybir.AluOpType
+ACT = mybir.ActivationFunctionType
+
+P = 128
+K = 2048
+PASSES = 4
+TOK_TILES = 4
+N_Q = 16
+N_KV = 4
+N_W = N_Q + 2 * N_KV
+HALF = 64
+ROPE_BASE = 10000.0
+RMS_EPS = 1.1920929e-07
+TWO_PI = 2.0 * math.pi
+
+LAG_T = 1
+LAG_Q = 2
+LAG_M = 3
+LAG_R = 4
+LAG_P = 5
+LAG_S = 6
+W_GROUPS = ((0,), (1,), (2, 3), (4, 5, 6, 7), (8, 9, 10, 11), (12, 13, 14, 15), (16, 17, 18, 19), (20, 21, 22, 23))
+
+
+def tile_causalselfattention_pa_kernel(
+    tc, x, w_qkv_tern_bytes, w_qkv_tern_scale, q_gain, out_0, out_1, out_2
+):
+    nc = tc.nc
+    with ExitStack() as ctx:
+        ctx.enter_context(tc.manual_schedule())
+        const = ctx.enter_context(tc.tile_pool(name="const", bufs=1))
+        wbp = ctx.enter_context(tc.tile_pool(name="wbp", bufs=3))
+        grpp = ctx.enter_context(tc.tile_pool(name="grpp", bufs=6))
+        codep = ctx.enter_context(tc.tile_pool(name="codep", bufs=3))
+        ropep = ctx.enter_context(tc.tile_pool(name="ropep", bufs=2))
+        outp = ctx.enter_context(tc.tile_pool(name="outp", bufs=3))
+        statp = ctx.enter_context(tc.tile_pool(name="statp", bufs=3))
+        tpp = ctx.enter_context(tc.psum_pool(name="tpp", bufs=3))
+        accp = ctx.enter_context(tc.psum_pool(name="accp", bufs=3))
+        zpp = ctx.enter_context(tc.psum_pool(name="zpp", bufs=2))
+
+        wby = {}
+        wgroup_tiles = []
+        for n, group in enumerate(W_GROUPS):
+            gt = const.tile([P, len(group), K], U8, name="wbytes%d" % n)
+            wgroup_tiles.append(gt)
+            for j, i in enumerate(group):
+                wby[i] = gt[:, j, :]
+
+        def load_group(n):
+            group = W_GROUPS[n]
+            rows = w_qkv_tern_bytes[group[0] * P : (group[-1] + 1) * P, :]
+            nc.sync.dma_start(out=wgroup_tiles[n][:], in_=rows.rearrange("(j p) k -> p j k", p=P))
+
+        xs = []
+        for a in range(TOK_TILES):
+            xs.append(const.tile([P, K], BF16, name="xrows%d" % a))
+        sbc = const.tile([P, K], F32, name="sbc")
+        gbf = const.tile([P, N_Q], BF16, name="gbf")
+
+        nc.sync.dma_start(
+            out=sbc[:], in_=w_qkv_tern_scale.rearrange("o k -> (o k)").partition_broadcast(P)
+        )
+        load_group(0)
+        for a in range(TOK_TILES):
+            nc.sync.dma_start(out=xs[a][:], in_=x[0, a * P : (a + 1) * P, :])
+        load_group(1)
+        load_group(2)
+        nc.sync.dma_start(out=gbf[:], in_=q_gain.partition_broadcast(P))
+        for n in range(3, len(W_GROUPS)):
+            load_group(n)
+
+        tok_i = const.tile([P, TOK_TILES], I32, name="tok_i")
+        nc.gpsimd.iota(tok_i[:], pattern=[[P, TOK_TILES]], base=0, channel_multiplier=1)
+        ident = const.tile([P, P], F32, name="ident")
+        make_identity(nc, ident[:])
+        swap = const.tile([P, P], F32, name="swap")
+        nc.gpsimd.tensor_copy(out=swap[:, 0:HALF], in_=ident[:, HALF:P])
+        nc.gpsimd.tensor_copy(out=swap[:, HALF:P], in_=ident[:, 0:HALF])
+
+        one = const.tile([P, 1], F32, name="one")
+        nc.vector.memset(one[:], 1.0)
+        eps = const.tile([P, 1], F32, name="eps")
+        nc.vector.memset(eps[:], RMS_EPS)
+        warm = const.tile([P, 1], F32, name="warm")
+        nc.scalar.activation(out=warm[:], in_=one[:], func=ACT.Sin)
+
+        turn = const.tile([P, HALF], F32, name="turn")
+        nc.vector.tensor_scalar(
+            out=turn[:, 0:1], in0=one[:], scalar1=1.0 / TWO_PI, scalar2=None, op0=ALU.mult
+        )
+        for e in range(6):
+            w = 2**e
+            nc.vector.tensor_scalar(
+                out=turn[:, w : 2 * w],
+                in0=turn[:, 0:w],
+                scalar1=ROPE_BASE ** (-w / 64.0),
+                scalar2=None,
+                op0=ALU.mult,
+            )
+        tok = const.tile([P, TOK_TILES], F32, name="tok")
+        nc.vector.tensor_copy(out=tok[:], in_=tok_i[:])
+        ang = const.tile([P, TOK_TILES, 2, HALF], F32, name="ang")
+        for a in range(TOK_TILES):
+            nc.vector.tensor_scalar(
+                out=ang[:, a, 1, :], in0=turn[:], scalar1=tok[:, a : a + 1], scalar2=None, op0=ALU.mult
+            )
+            nc.vector.tensor_scalar(
+                out=ang[:, a, 0, :],
+                in0=turn[:],
+                scalar1=tok[:, a : a + 1],
+                scalar2=0.25,
+                op0=ALU.mult,
+                op1=ALU.add,
+            )
+        ang_flat = ang[:].rearrange("p a c j -> p (a c j)")
+        whole = const.tile([P, 512], I32, name="whole")
+        nc.vector.tensor_copy(out=whole[:], in_=ang_flat)
+        frac = const.tile([P, 512], F32, name="frac")
+        nc.vector.tensor_tensor(out=frac[:], in0=ang_flat, in1=whole[:], op=ALU.subtract)
+        nfrac = const.tile([P, TOK_TILES, 2, HALF], F32, name="nfrac")
+        nc.vector.scalar_tensor_tensor(
+            out=nfrac[:].rearrange("p a c j -> p (a c j)"),
+            in0=frac[:],
+            scalar=0.5,
+            in1=frac[:],
+            op0=ALU.is_gt,
+            op1=ALU.subtract,
+        )
+        cos_t = const.tile([P, TOK_TILES, P], F32, name="cos_t")
+        sin_t = const.tile([P, TOK_TILES, P], F32, name="sin_t")
+        nc.scalar.activation(out=cos_t[:, :, 0:HALF], in_=nfrac[:, :, 0, :], func=ACT.Sin, scale=-TWO_PI)
+        nc.scalar.activation(out=cos_t[:, :, HALF:P], in_=nfrac[:, :, 0, :], func=ACT.Sin, scale=-TWO_PI)
+        nc.scalar.activation(out=sin_t[:, :, 0:HALF], in_=nfrac[:, :, 1, :], func=ACT.Sin, scale=TWO_PI)
+        nc.scalar.activation(out=sin_t[:, :, HALF:P], in_=nfrac[:, :, 1, :], func=ACT.Sin, scale=-TWO_PI)
+        nc.scalar.activation(
+            out=warm[:], in_=one[:], func=ACT.Abs_reciprocal_sqrt, scale=1.0 / P, bias=eps[:]
+        )
+        gf = const.tile([P, N_Q], F32, name="gf")
+
+        cos_c = const.tile([P, 512], F32, name="cos_c")
+        sin_c = const.tile([P, 512], F32, name="sin_c")
+        xgrp = const.tile([P, 4096], F32, name="xgrp", align_bytes=64)
+        xc = const.tile([P, 2048], U32, name="xcodes", align_bytes=64)
+        xsc = const.tile([P, 2048], U8, name="xscales", align_bytes=64)
+
+        wide = {}
+        banks = {}
+        grps = {}
+        wcodes = {}
+        accs = {}
+        ropes = {}
+        zs = {}
+        stats = {}
+
+        q_view = out_0.rearrange("o (a p) h d -> p (o a) h d", p=P)
+        k_view = out_1.rearrange("o (a p) h d -> p (o a) h d", p=P)
+        v_view = out_2.rearrange("o (a p) h d -> p (o a) h d", p=P)
+
+        def widen(i):
+            wb = wbp.tile([P, K], BF16, name="wb", align_bytes=64)
+            nc.vector.tensor_tensor(out=wb[:], in0=wby[i].bitcast(FP8), in1=sbc[:], op=ALU.mult)
+            wide[i] = wb
+
+        def table_transposes():
+            for src, dst in ((cos_t, cos_c), (sin_t, sin_c)):
+                tp = tpp.tile([P, 4, P], F32, name="tp")
+                for a in range(TOK_TILES):
+                    nc.tensor.transpose(tp[:, a, :], src[:, a, :], ident[:])
+                nc.scalar.copy(out=dst[:], in_=tp[:].rearrange("p a t -> p (a t)"))
+
+        def transposes(key, rows):
+            words = rows[:].bitcast(F32)
+            pair = []
+            for b in range(2):
+                tp = tpp.tile([P, 4, P], F32, name="tp")
+                for gg in range(2):
+                    g = 2 * b + gg
+                    for u in range(2):
+                        nc.tensor.transpose(
+                            tp[:, 2 * gg + u, :], words[:, 256 * g + u : 256 * (g + 1) : 2], ident[:]
+                        )
+                pair.append(tp)
+            banks[key] = pair
+
+        def evacuate_w(i, b):
+            if not 0 <= i < N_W:
+                return
+            if b == 0:
+                grps[i] = grpp.tile([P, 1024], F32, name="grp", align_bytes=64)
+            nc.scalar.copy(
+                out=grps[i][:, 512 * b : 512 * (b + 1)].rearrange("p (g r u) -> p g r u", g=2, u=2),
+                in_=banks[i][b][:].rearrange("p (g u) r -> p g r u", u=2),
+            )
+
+        def evacuate_x(a):
+            view = xgrp[:].rearrange("p (g a r u) -> p g a r u", g=PASSES, a=TOK_TILES, u=2)
+            for b in range(2):
+                nc.scalar.copy(
+                    out=view[:, 2 * b : 2 * b + 2, a, :, :],
+                    in_=banks["x%d" % a][b][:].rearrange("p (g u) r -> p g r u", u=2),
+                )
+
+        def quantise_x(g):
+            nc.vector.quantize_mx(
+                out=xc[:, 512 * g : 512 * (g + 1)].bitcast(FP8X4),
+                scales=xsc[:, 512 * g : 512 * (g + 1)],
+                in_=xgrp[:, 1024 * g : 1024 * (g + 1)].bitcast(BF16),
+            )
+
+        def quantise_w(i):
+            codes = codep.tile([P, 512], U32, name="wcodes", align_bytes=64)
+            scales = codep.tile([P, 512], U8, name="wscales", align_bytes=64)
+            nc.vector.quantize_mx(
+                out=codes[:].bitcast(FP8X4), scales=scales[:], in_=grps[i][:].bitcast(BF16)
+            )
+            wcodes[i] = (codes, scales)
+
+        def matmuls_qk(i, part):
+            codes, scales = wcodes[i]
+            if part == 0:
+                accs[i] = accp.tile([P, 512], F32, name="acc")
+            acc = accs[i]
+            for g in (2 * part, 2 * part + 1):
+                wcols = slice(P * g, P * (g + 1))
+                xcols = slice(512 * g, 512 * (g + 1))
+                nc.tensor.matmul_mx(
+                    out=acc[:],
+                    lhsT=codes[:, wcols].bitcast(FP8X4),
+                    lhsT_scale=scales[:, wcols],
+                    rhs=xc[:, xcols].bitcast(FP8X4),
+                    rhs_scale=xsc[:, xcols],
+                    start=(g == 0),
+                    stop=(g == PASSES - 1),
+                )
+
+        def matmuls_v(i, part):
+            codes, scales = wcodes[i]
+            if part == 0:
+                accs[i] = accp.tile([P, 512], F32, name="acc")
+            acc = accs[i]
+            for a in (2 * part, 2 * part + 1):
+                for g in range(PASSES):
+                    wcols = slice(P * g, P * (g + 1))
+                    xcols = slice(512 * g + P * a, 512 * g + P * (a + 1))
+                    nc.tensor.matmul_mx(
+                        out=acc[:, P * a : P * (a + 1)],
+                        lhsT=xc[:, xcols].bitcast(FP8X4),
+                        lhsT_scale=xsc[:, xcols],
+                        rhs=codes[:, wcols].bitcast(FP8X4),
+                        rhs_scale=scales[:, wcols],
+                        start=(g == 0),
+                        stop=(g == PASSES - 1),
+                    )
+
+        def matmuls(i, part):
+            if 0 <= i < N_Q + N_KV:
+                matmuls_qk(i, part)
+            elif i < N_W and i >= 0:
+                matmuls_v(i, part)
+
+        def rope_products(i):
+            ra = ropep.tile([P, 512], F32, name="ra")
+            rt = ropep.tile([P, 512], F32, name="rt")
+            nc.vector.tensor_tensor(out=rt[:], in0=accs[i][:], in1=sin_c[:], op=ALU.mult)
+            nc.vector.tensor_tensor(out=ra[:], in0=accs[i][:], in1=cos_c[:], op=ALU.mult)
+            ropes[i] = (ra, rt)
+
+        def rope_sum(i):
+            ra, rt = ropes[i]
+            z = zpp.tile([P, TOK_TILES, P], F32, name="z")
+            for a in range(TOK_TILES):
+                blk = slice(P * a, P * (a + 1))
+                nc.tensor.matmul(
+                    z[:, a, :], lhsT=ra[:, blk], rhs=ident[:], is_transpose=True, start=True, stop=False
+                )
+                nc.tensor.matmul(
+                    z[:, a, :], lhsT=rt[:, blk], rhs=swap[:], is_transpose=True, start=False, stop=True
+                )
+            zs[i] = z
+
+        def is_qk(i):
+            return 0 <= i < N_Q + N_KV
+
+        def norm_squares(i):
+            if not is_qk(i):
+                return
+            junk = statp.tile([P, P], BF16, name="junk")
+            ss = statp.tile([P, TOK_TILES], F32, name="ss")
+            for a in range(TOK_TILES):
+                nc.scalar.activation(
+                    out=junk[:], in_=zs[i][:, a, :], func=ACT.Square, accum_out=ss[:, a : a + 1]
+                )
+            stats[i] = ss
+
+        def norm_rsqrt(i):
+            if not is_qk(i):
+                return
+            rs = statp.tile([P, TOK_TILES], F32, name="rs")
+            nc.scalar.activation(
+                out=rs[:], in_=stats[i][:], func=ACT.Abs_reciprocal_sqrt, scale=1.0 / P, bias=eps[:]
+            )
+            stats[i] = rs
+
+        def norm_gain(i):
+            if not 0 <= i < N_Q:
+                return
+            rg = statp.tile([P, TOK_TILES], F32, name="rg")
+            nc.scalar.activation(out=rg[:], in_=stats[i][:], func=ACT.Copy, scale=gf[:, i : i + 1])
+            stats[i] = rg
+
+        def norm_apply(i):
+            if not is_qk(i):
+                return
+            o = outp.tile([P, TOK_TILES, P], F32, name="o")
+            for a in range(TOK_TILES):
+                nc.scalar.activation(
+                    out=o[:, a, :], in_=zs[i][:, a, :], func=ACT.Copy, scale=stats[i][:, a : a + 1]
+                )
+            if i < N_Q:
+                nc.sync.dma_start(out=q_view[:, :, i, :], in_=o[:])
+            else:
+                nc.sync.dma_start(out=k_view[:, :, i - N_Q, :], in_=o[:])
+
+        def post_v(i):
+            o = outp.tile([P, TOK_TILES, P], F32, name="o")
+            nc.scalar.copy(out=o[:].rearrange("p a d -> p (a d)"), in_=accs[i][:])
+            nc.sync.dma_start(out=v_view[:, :, i - N_Q - N_KV, :], in_=o[:])
+
+        n_qk = N_Q + N_KV
+        for s in range(N_W + LAG_S + 1):
+            if s < N_W:
+                widen(s)
+            if s < 2:
+                for a in (2 * s, 2 * s + 1):
+                    transposes("x%d" % a, xs[a])
+            if s == 2:
+                table_transposes()
+                nc.scalar.copy(out=gf[:], in_=gbf[:])
+            if 0 <= s - LAG_T < N_W:
+                transposes(s - LAG_T, wide[s - LAG_T])
+            matmuls(s - LAG_M, 0)
+            if 0 <= s - LAG_P < n_qk:
+                rope_sum(s - LAG_P)
+            matmuls(s - LAG_M, 1)
+            if s < 2:
+                for a in (2 * s, 2 * s + 1):
+                    evacuate_x(a)
+            norm_rsqrt(s - LAG_S)
+            evacuate_w(s - LAG_T, 0)
+            norm_gain(s - LAG_S)
+            evacuate_w(s - LAG_T, 1)
+            norm_apply(s - LAG_S)
+            norm_squares(s - LAG_P)
+            if n_qk <= s - LAG_M < N_W:
+                post_v(s - LAG_M)
+            if s == 2:
+                for g in range(PASSES):
+                    quantise_x(g)
+            if 0 <= s - LAG_Q < N_W:
+                quantise_w(s - LAG_Q)
+            if 0 <= s - LAG_R < n_qk:
+                rope_products(s - LAG_R)

@@ -34,6 +34,7 @@ LAG_M = 3
 LAG_R = 4
 LAG_P = 5
 LAG_S = 6
+V_COLS = 256
 W_GROUPS = ((0,), (1,), (2, 3), (4, 5, 6, 7), (8, 9, 10, 11), (12, 13, 14, 15), (16, 17, 18, 19), (20, 21, 22, 23))
 
 
@@ -50,6 +51,7 @@ def tile_causalselfattention_pa_kernel(
         ropep = ctx.enter_context(tc.tile_pool(name="ropep", bufs=2))
         outp = ctx.enter_context(tc.tile_pool(name="outp", bufs=3))
         statp = ctx.enter_context(tc.tile_pool(name="statp", bufs=3))
+        ugp = ctx.enter_context(tc.tile_pool(name="ugp", bufs=3))
         tpp = ctx.enter_context(tc.psum_pool(name="tpp", bufs=3))
         accp = ctx.enter_context(tc.psum_pool(name="accp", bufs=3))
         zpp = ctx.enter_context(tc.psum_pool(name="zpp", bufs=2))
@@ -167,6 +169,8 @@ def tile_causalselfattention_pa_kernel(
         ropes = {}
         zs = {}
         stats = {}
+        uas = {}
+        gparts = {}
 
         q_view = out_0.rearrange("o (a p) h d -> p (o a) h d", p=P)
         k_view = out_1.rearrange("o (a p) h d -> p (o a) h d", p=P)
@@ -226,9 +230,12 @@ def tile_causalselfattention_pa_kernel(
         def quantise_w(i):
             codes = codep.tile([P, 512], U32, name="wcodes", align_bytes=64)
             scales = codep.tile([P, 512], U8, name="wscales", align_bytes=64)
-            nc.vector.quantize_mx(
-                out=codes[:].bitcast(FP8X4), scales=scales[:], in_=grps[i][:].bitcast(BF16)
-            )
+            for b in range(2):
+                nc.vector.quantize_mx(
+                    out=codes[:, 256 * b : 256 * (b + 1)].bitcast(FP8X4),
+                    scales=scales[:, 256 * b : 256 * (b + 1)],
+                    in_=grps[i][:, 512 * b : 512 * (b + 1)].bitcast(BF16),
+                )
             wcodes[i] = (codes, scales)
 
         def matmuls_qk(i, part):
@@ -274,11 +281,25 @@ def tile_causalselfattention_pa_kernel(
             elif i < N_W and i >= 0:
                 matmuls_v(i, part)
 
+        def rope_copy(i):
+            if not is_qk(i):
+                return
+            ua = ugp.tile([P, 512 - V_COLS], F32, name="ua")
+            nc.scalar.copy(out=ua[:], in_=accs[i][:, V_COLS:512])
+            uas[i] = ua
+
+        def rope_gpsimd(i, spent):
+            rtg = grps[spent][:, 0 : 512 - V_COLS]
+            nc.gpsimd.tensor_tensor(out=rtg, in0=uas[i][:], in1=sin_c[:, V_COLS:512], op=ALU.mult)
+            gparts[i] = rtg
+
         def rope_products(i):
             ra = ropep.tile([P, 512], F32, name="ra")
-            rt = ropep.tile([P, 512], F32, name="rt")
-            nc.vector.tensor_tensor(out=rt[:], in0=accs[i][:], in1=sin_c[:], op=ALU.mult)
+            rt = ropep.tile([P, V_COLS], F32, name="rt")
             nc.vector.tensor_tensor(out=ra[:], in0=accs[i][:], in1=cos_c[:], op=ALU.mult)
+            nc.vector.tensor_tensor(
+                out=rt[:], in0=accs[i][:, 0:V_COLS], in1=sin_c[:, 0:V_COLS], op=ALU.mult
+            )
             ropes[i] = (ra, rt)
 
         def rope_sum(i):
@@ -289,8 +310,12 @@ def tile_causalselfattention_pa_kernel(
                 nc.tensor.matmul(
                     z[:, a, :], lhsT=ra[:, blk], rhs=ident[:], is_transpose=True, start=True, stop=False
                 )
+                if P * a < V_COLS:
+                    sine = rt[:, blk]
+                else:
+                    sine = gparts[i][:, P * a - V_COLS : P * (a + 1) - V_COLS]
                 nc.tensor.matmul(
-                    z[:, a, :], lhsT=rt[:, blk], rhs=swap[:], is_transpose=True, start=False, stop=True
+                    z[:, a, :], lhsT=sine, rhs=swap[:], is_transpose=True, start=False, stop=True
                 )
             zs[i] = z
 
@@ -365,6 +390,7 @@ def tile_causalselfattention_pa_kernel(
             evacuate_w(s - LAG_T, 0)
             norm_gain(s - LAG_S)
             evacuate_w(s - LAG_T, 1)
+            rope_copy(s - LAG_R)
             norm_apply(s - LAG_S)
             norm_squares(s - LAG_P)
             if n_qk <= s - LAG_M < N_W:
@@ -375,4 +401,5 @@ def tile_causalselfattention_pa_kernel(
             if 0 <= s - LAG_Q < N_W:
                 quantise_w(s - LAG_Q)
             if 0 <= s - LAG_R < n_qk:
+                rope_gpsimd(s - LAG_R, s - LAG_Q)
                 rope_products(s - LAG_R)

@@ -34,7 +34,7 @@ LAG_M = 3
 LAG_R = 4
 LAG_P = 5
 LAG_S = 6
-V_COLS = 256
+V_COLS = 384
 W_GROUPS = ((0,), (1,), (2, 3), (4, 5, 6, 7), (8, 9, 10, 11), (12, 13, 14, 15), (16, 17, 18, 19), (20, 21, 22, 23))
 
 
@@ -49,7 +49,7 @@ def tile_causalselfattention_pa_kernel(
         grpp = ctx.enter_context(tc.tile_pool(name="grpp", bufs=6))
         codep = ctx.enter_context(tc.tile_pool(name="codep", bufs=3))
         ropep = ctx.enter_context(tc.tile_pool(name="ropep", bufs=2))
-        outp = ctx.enter_context(tc.tile_pool(name="outp", bufs=3))
+        outp = ctx.enter_context(tc.tile_pool(name="outp", bufs=6))
         statp = ctx.enter_context(tc.tile_pool(name="statp", bufs=3))
         ugp = ctx.enter_context(tc.tile_pool(name="ugp", bufs=3))
         tpp = ctx.enter_context(tc.psum_pool(name="tpp", bufs=3))
@@ -155,8 +155,7 @@ def tile_causalselfattention_pa_kernel(
         )
         gf = const.tile([P, N_Q], F32, name="gf")
 
-        cos_c = const.tile([P, 512], F32, name="cos_c")
-        sin_c = const.tile([P, 512], F32, name="sin_c")
+        cs_c = const.tile([P, 2, 512], F32, name="cs_c")
         xgrp = const.tile([P, 4096], F32, name="xgrp", align_bytes=64)
         xc = const.tile([P, 2048], U32, name="xcodes", align_bytes=64)
         xsc = const.tile([P, 2048], U8, name="xscales", align_bytes=64)
@@ -182,11 +181,11 @@ def tile_causalselfattention_pa_kernel(
             wide[i] = wb
 
         def table_transposes():
-            for src, dst in ((cos_t, cos_c), (sin_t, sin_c)):
+            for src, dst in ((cos_t, cs_c[:, 0, :]), (sin_t, cs_c[:, 1, :])):
                 tp = tpp.tile([P, 4, P], F32, name="tp")
                 for a in range(TOK_TILES):
                     nc.tensor.transpose(tp[:, a, :], src[:, a, :], ident[:])
-                nc.scalar.copy(out=dst[:], in_=tp[:].rearrange("p a t -> p (a t)"))
+                nc.scalar.copy(out=dst, in_=tp[:].rearrange("p a t -> p (a t)"))
 
         def transposes(key, rows):
             words = rows[:].bitcast(F32)
@@ -284,38 +283,39 @@ def tile_causalselfattention_pa_kernel(
         def rope_copy(i):
             if not is_qk(i):
                 return
-            ua = ugp.tile([P, 512 - V_COLS], F32, name="ua")
-            nc.scalar.copy(out=ua[:], in_=accs[i][:, V_COLS:512])
+            ua = ugp.tile([P, 2, 512 - V_COLS], F32, name="ua")
+            nc.scalar.copy(
+                out=ua[:], in_=accs[i][:, V_COLS:512].unsqueeze(1).to_broadcast([P, 2, 512 - V_COLS])
+            )
             uas[i] = ua
 
         def rope_gpsimd(i, spent):
-            rtg = grps[spent][:, 0 : 512 - V_COLS]
-            nc.gpsimd.tensor_tensor(out=rtg, in0=uas[i][:], in1=sin_c[:, V_COLS:512], op=ALU.mult)
-            gparts[i] = rtg
+            part = grps[spent][:, 0 : 2 * (512 - V_COLS)].rearrange("p (c t) -> p c t", c=2)
+            nc.gpsimd.tensor_tensor(out=part, in0=uas[i][:], in1=cs_c[:, :, V_COLS:512], op=ALU.mult)
+            gparts[i] = part
 
         def rope_products(i):
-            ra = ropep.tile([P, 512], F32, name="ra")
-            rt = ropep.tile([P, V_COLS], F32, name="rt")
-            nc.vector.tensor_tensor(out=ra[:], in0=accs[i][:], in1=cos_c[:], op=ALU.mult)
+            rr = ropep.tile([P, 2, V_COLS], F32, name="rr")
             nc.vector.tensor_tensor(
-                out=rt[:], in0=accs[i][:, 0:V_COLS], in1=sin_c[:, 0:V_COLS], op=ALU.mult
+                out=rr[:],
+                in0=accs[i][:, 0:V_COLS].unsqueeze(1).to_broadcast([P, 2, V_COLS]),
+                in1=cs_c[:, :, 0:V_COLS],
+                op=ALU.mult,
             )
-            ropes[i] = (ra, rt)
+            ropes[i] = rr
 
         def rope_sum(i):
-            ra, rt = ropes[i]
             z = zpp.tile([P, TOK_TILES, P], F32, name="z")
             for a in range(TOK_TILES):
-                blk = slice(P * a, P * (a + 1))
-                nc.tensor.matmul(
-                    z[:, a, :], lhsT=ra[:, blk], rhs=ident[:], is_transpose=True, start=True, stop=False
-                )
                 if P * a < V_COLS:
-                    sine = rt[:, blk]
+                    both = ropes[i][:, :, P * a : P * (a + 1)]
                 else:
-                    sine = gparts[i][:, P * a - V_COLS : P * (a + 1) - V_COLS]
+                    both = gparts[i][:, :, P * a - V_COLS : P * (a + 1) - V_COLS]
                 nc.tensor.matmul(
-                    z[:, a, :], lhsT=sine, rhs=swap[:], is_transpose=True, start=False, stop=True
+                    z[:, a, :], lhsT=both[:, 0, :], rhs=ident[:], is_transpose=True, start=True, stop=False
+                )
+                nc.tensor.matmul(
+                    z[:, a, :], lhsT=both[:, 1, :], rhs=swap[:], is_transpose=True, start=False, stop=True
                 )
             zs[i] = z
 
@@ -386,10 +386,10 @@ def tile_causalselfattention_pa_kernel(
             if s < 2:
                 for a in (2 * s, 2 * s + 1):
                     evacuate_x(a)
-            norm_rsqrt(s - LAG_S)
             evacuate_w(s - LAG_T, 0)
-            norm_gain(s - LAG_S)
+            norm_rsqrt(s - LAG_S)
             evacuate_w(s - LAG_T, 1)
+            norm_gain(s - LAG_S)
             rope_copy(s - LAG_R)
             norm_apply(s - LAG_S)
             norm_squares(s - LAG_P)

@@ -390,9 +390,9 @@ def tile_causalselfattention_pa_kernel(
             norm_rsqrt(s - LAG_S)
             evacuate_w(s - LAG_T, 1)
             norm_gain(s - LAG_S)
-            rope_copy(s - LAG_R)
             norm_apply(s - LAG_S)
             norm_squares(s - LAG_P)
+            rope_copy(s - LAG_M)
             if n_qk <= s - LAG_M < N_W:
                 post_v(s - LAG_M)
             if s == 2:

@@ -386,10 +386,10 @@ def tile_causalselfattention_pa_kernel(
             if s < 2:
                 for a in (2 * s, 2 * s + 1):
                     evacuate_x(a)
-            evacuate_w(s - LAG_T, 0)
             norm_rsqrt(s - LAG_S)
-            evacuate_w(s - LAG_T, 1)
+            evacuate_w(s - LAG_T, 0)
             norm_gain(s - LAG_S)
+            evacuate_w(s - LAG_T, 1)
             norm_apply(s - LAG_S)
             norm_squares(s - LAG_P)
             rope_copy(s - LAG_M)

from contextlib import ExitStack
import math

import concourse.mybir as mybir
from concourse.masks import make_identity

FLOPS = 2 * 512 * 3072 * 2048

F32 = mybir.dt.float32
BF16 = mybir.dt.bfloat16
I32 = mybir.dt.int32
U32 = mybir.dt.uint32
U8 = mybir.dt.uint8
FP8 = mybir.dt.float8_e4m3fn
FP8X4 = mybir.dt.float8_e4m3fn_x4
ALU = mybir.AluOpType
ACT = mybir.ActivationFunctionType

P = 128
K = 2048
PASSES = 4
TOK_TILES = 4
N_Q = 16
N_KV = 4
N_W = N_Q + 2 * N_KV
HALF = 64
ROPE_BASE = 10000.0
RMS_EPS = 1.1920929e-07
TWO_PI = 2.0 * math.pi

LAG_T = 1
LAG_Q = 2
LAG_M = 3
LAG_R = 4
LAG_P = 5
LAG_S = 6
V_COLS = 384
W_GROUPS = ((0,), (1,), (2, 3), (4, 5, 6, 7), (8, 9, 10, 11), (12, 13, 14, 15), (16, 17, 18, 19), (20, 21, 22, 23))


def tile_causalselfattention_pa_kernel(
    tc, x, w_qkv_tern_bytes, w_qkv_tern_scale, q_gain, out_0, out_1, out_2
):
    nc = tc.nc
    with ExitStack() as ctx:
        ctx.enter_context(tc.manual_schedule())
        const = ctx.enter_context(tc.tile_pool(name="const", bufs=1))
        wbp = ctx.enter_context(tc.tile_pool(name="wbp", bufs=3))
        grpp = ctx.enter_context(tc.tile_pool(name="grpp", bufs=6))
        codep = ctx.enter_context(tc.tile_pool(name="codep", bufs=3))
        ropep = ctx.enter_context(tc.tile_pool(name="ropep", bufs=2))
        outp = ctx.enter_context(tc.tile_pool(name="outp", bufs=6))
        statp = ctx.enter_context(tc.tile_pool(name="statp", bufs=3))
        ugp = ctx.enter_context(tc.tile_pool(name="ugp", bufs=3))
        tpp = ctx.enter_context(tc.psum_pool(name="tpp", bufs=3))
        accp = ctx.enter_context(tc.psum_pool(name="accp", bufs=3))
        zpp = ctx.enter_context(tc.psum_pool(name="zpp", bufs=2))

        wby = {}
        wgroup_tiles = []
        for n, group in enumerate(W_GROUPS):
            gt = const.tile([P, len(group), K], U8, name="wbytes%d" % n)
            wgroup_tiles.append(gt)
            for j, i in enumerate(group):
                wby[i] = gt[:, j, :]

        def load_group(n):
            group = W_GROUPS[n]
            rows = w_qkv_tern_bytes[group[0] * P : (group[-1] + 1) * P, :]
            nc.sync.dma_start(out=wgroup_tiles[n][:], in_=rows.rearrange("(j p) k -> p j k", p=P))

        xs = []
        for a in range(TOK_TILES):
            xs.append(const.tile([P, K], BF16, name="xrows%d" % a))
        sbc = const.tile([P, K], F32, name="sbc")
        gbf = const.tile([P, N_Q], BF16, name="gbf")

        nc.sync.dma_start(
            out=sbc[:], in_=w_qkv_tern_scale.rearrange("o k -> (o k)").partition_broadcast(P)
        )
        load_group(0)
        for a in range(TOK_TILES):
            nc.sync.dma_start(out=xs[a][:], in_=x[0, a * P : (a + 1) * P, :])
        load_group(1)
        load_group(2)
        nc.sync.dma_start(out=gbf[:], in_=q_gain.partition_broadcast(P))
        for n in range(3, len(W_GROUPS)):
            load_group(n)

        tok_i = const.tile([P, TOK_TILES], I32, name="tok_i")
        nc.gpsimd.iota(tok_i[:], pattern=[[P, TOK_TILES]], base=0, channel_multiplier=1)
        ident = const.tile([P, P], F32, name="ident")
        make_identity(nc, ident[:])
        swap = const.tile([P, P], F32, name="swap")
        nc.gpsimd.tensor_copy(out=swap[:, 0:HALF], in_=ident[:, HALF:P])
        nc.gpsimd.tensor_copy(out=swap[:, HALF:P], in_=ident[:, 0:HALF])

        one = const.tile([P, 1], F32, name="one")
        nc.vector.memset(one[:], 1.0)
        eps = const.tile([P, 1], F32, name="eps")
        nc.vector.memset(eps[:], RMS_EPS)
        warm = const.tile([P, 1], F32, name="warm")
        nc.scalar.activation(out=warm[:], in_=one[:], func=ACT.Sin)

        turn = const.tile([P, HALF], F32, name="turn")
        nc.vector.tensor_scalar(
            out=turn[:, 0:1], in0=one[:], scalar1=1.0 / TWO_PI, scalar2=None, op0=ALU.mult
        )
        for e in range(6):
            w = 2**e
            nc.vector.tensor_scalar(
                out=turn[:, w : 2 * w],
                in0=turn[:, 0:w],
                scalar1=ROPE_BASE ** (-w / 64.0),
                scalar2=None,
                op0=ALU.mult,
            )
        tok = const.tile([P, TOK_TILES], F32, name="tok")
        nc.vector.tensor_copy(out=tok[:], in_=tok_i[:])
        ang = const.tile([P, TOK_TILES, 2, HALF], F32, name="ang")
        for a in range(TOK_TILES):
            nc.vector.tensor_scalar(
                out=ang[:, a, 1, :], in0=turn[:], scalar1=tok[:, a : a + 1], scalar2=None, op0=ALU.mult
            )
            nc.vector.tensor_scalar(
                out=ang[:, a, 0, :],
                in0=turn[:],
                scalar1=tok[:, a : a + 1],
                scalar2=0.25,
                op0=ALU.mult,
                op1=ALU.add,
            )
        ang_flat = ang[:].rearrange("p a c j -> p (a c j)")
        whole = const.tile([P, 512], I32, name="whole")
        nc.vector.tensor_copy(out=whole[:], in_=ang_flat)
        frac = const.tile([P, 512], F32, name="frac")
        nc.vector.tensor_tensor(out=frac[:], in0=ang_flat, in1=whole[:], op=ALU.subtract)
        nfrac = const.tile([P, TOK_TILES, 2, HALF], F32, name="nfrac")
        nc.vector.scalar_tensor_tensor(
            out=nfrac[:].rearrange("p a c j -> p (a c j)"),
            in0=frac[:],
            scalar=0.5,
            in1=frac[:],
            op0=ALU.is_gt,
            op1=ALU.subtract,
        )
        cos_t = const.tile([P, TOK_TILES, P], F32, name="cos_t")
        sin_t = const.tile([P, TOK_TILES, P], F32, name="sin_t")
        nc.scalar.activation(out=cos_t[:, :, 0:HALF], in_=nfrac[:, :, 0, :], func=ACT.Sin, scale=-TWO_PI)
        nc.scalar.activation(out=cos_t[:, :, HALF:P], in_=nfrac[:, :, 0, :], func=ACT.Sin, scale=-TWO_PI)
        nc.scalar.activation(out=sin_t[:, :, 0:HALF], in_=nfrac[:, :, 1, :], func=ACT.Sin, scale=TWO_PI)
        nc.scalar.activation(out=sin_t[:, :, HALF:P], in_=nfrac[:, :, 1, :], func=ACT.Sin, scale=-TWO_PI)
        nc.scalar.activation(
            out=warm[:], in_=one[:], func=ACT.Abs_reciprocal_sqrt, scale=1.0 / P, bias=eps[:]
        )
        gf = const.tile([P, N_Q], F32, name="gf")

        cs_c = const.tile([P, 2, 512], F32, name="cs_c")
        xgrp = const.tile([P, 4096], F32, name="xgrp", align_bytes=64)
        xc = const.tile([P, 2048], U32, name="xcodes", align_bytes=64)
        xsc = const.tile([P, 2048], U8, name="xscales", align_bytes=64)

        wide = {}
        banks = {}
        grps = {}
        wcodes = {}
        accs = {}
        ropes = {}
        zs = {}
        stats = {}
        uas = {}
        gparts = {}

        q_view = out_0.rearrange("o (a p) h d -> p (o a) h d", p=P)
        k_view = out_1.rearrange("o (a p) h d -> p (o a) h d", p=P)
        v_view = out_2.rearrange("o (a p) h d -> p (o a) h d", p=P)

        def widen(i):
            wb = wbp.tile([P, K], BF16, name="wb", align_bytes=64)
            nc.vector.tensor_tensor(out=wb[:], in0=wby[i].bitcast(FP8), in1=sbc[:], op=ALU.mult)
            wide[i] = wb

        def table_transposes():
            for src, dst in ((cos_t, cs_c[:, 0, :]), (sin_t, cs_c[:, 1, :])):
                tp = tpp.tile([P, 4, P], F32, name="tp")
                for a in range(TOK_TILES):
                    nc.tensor.transpose(tp[:, a, :], src[:, a, :], ident[:])
                nc.scalar.copy(out=dst, in_=tp[:].rearrange("p a t -> p (a t)"))

        def transposes(key, rows):
            words = rows[:].bitcast(F32)
            pair = []
            for b in range(2):
                tp = tpp.tile([P, 4, P], F32, name="tp")
                for gg in range(2):
                    g = 2 * b + gg
                    for u in range(2):
                        nc.tensor.transpose(
                            tp[:, 2 * gg + u, :], words[:, 256 * g + u : 256 * (g + 1) : 2], ident[:]
                        )
                pair.append(tp)
            banks[key] = pair

        def evacuate_w(i, b):
            if not 0 <= i < N_W:
                return
            if b == 0:
                grps[i] = grpp.tile([P, 1024], F32, name="grp", align_bytes=64)
            nc.scalar.copy(
                out=grps[i][:, 512 * b : 512 * (b + 1)].rearrange("p (g r u) -> p g r u", g=2, u=2),
                in_=banks[i][b][:].rearrange("p (g u) r -> p g r u", u=2),
            )

        def evacuate_x(a):
            view = xgrp[:].rearrange("p (g a r u) -> p g a r u", g=PASSES, a=TOK_TILES, u=2)
            for b in range(2):
                nc.scalar.copy(
                    out=view[:, 2 * b : 2 * b + 2, a, :, :],
                    in_=banks["x%d" % a][b][:].rearrange("p (g u) r -> p g r u", u=2),
                )

        def quantise_x(g):
            nc.vector.quantize_mx(
                out=xc[:, 512 * g : 512 * (g + 1)].bitcast(FP8X4),
                scales=xsc[:, 512 * g : 512 * (g + 1)],
                in_=xgrp[:, 1024 * g : 1024 * (g + 1)].bitcast(BF16),
            )

        def quantise_w(i):
            codes = codep.tile([P, 512], U32, name="wcodes", align_bytes=64)
            scales = codep.tile([P, 512], U8, name="wscales", align_bytes=64)
            for b in range(2):
                nc.vector.quantize_mx(
                    out=codes[:, 256 * b : 256 * (b + 1)].bitcast(FP8X4),
                    scales=scales[:, 256 * b : 256 * (b + 1)],
                    in_=grps[i][:, 512 * b : 512 * (b + 1)].bitcast(BF16),
                )
            wcodes[i] = (codes, scales)

        def matmuls_qk(i, part):
            codes, scales = wcodes[i]
            if part == 0:
                accs[i] = accp.tile([P, 512], F32, name="acc")
            acc = accs[i]
            for g in (2 * part, 2 * part + 1):
                wcols = slice(P * g, P * (g + 1))
                xcols = slice(512 * g, 512 * (g + 1))
                nc.tensor.matmul_mx(
                    out=acc[:],
                    lhsT=codes[:, wcols].bitcast(FP8X4),
                    lhsT_scale=scales[:, wcols],
                    rhs=xc[:, xcols].bitcast(FP8X4),
                    rhs_scale=xsc[:, xcols],
                    start=(g == 0),
                    stop=(g == PASSES - 1),
                )

        def matmuls_v(i, part):
            codes, scales = wcodes[i]
            if part == 0:
                accs[i] = accp.tile([P, 512], F32, name="acc")
            acc = accs[i]
            for a in (2 * part, 2 * part + 1):
                for g in range(PASSES):
                    wcols = slice(P * g, P * (g + 1))
                    xcols = slice(512 * g + P * a, 512 * g + P * (a + 1))
                    nc.tensor.matmul_mx(
                        out=acc[:, P * a : P * (a + 1)],
                        lhsT=xc[:, xcols].bitcast(FP8X4),
                        lhsT_scale=xsc[:, xcols],
                        rhs=codes[:, wcols].bitcast(FP8X4),
                        rhs_scale=scales[:, wcols],
                        start=(g == 0),
                        stop=(g == PASSES - 1),
                    )

        def matmuls(i, part):
            if 0 <= i < N_Q + N_KV:
                matmuls_qk(i, part)
            elif i < N_W and i >= 0:
                matmuls_v(i, part)

        def rope_copy(i):
            if not is_qk(i):
                return
            ua = ugp.tile([P, 2, 512 - V_COLS], F32, name="ua")
            nc.scalar.copy(
                out=ua[:], in_=accs[i][:, V_COLS:512].unsqueeze(1).to_broadcast([P, 2, 512 - V_COLS])
            )
            uas[i] = ua

        def rope_gpsimd(i, spent):
            part = grps[spent][:, 0 : 2 * (512 - V_COLS)].rearrange("p (c t) -> p c t", c=2)
            nc.gpsimd.tensor_tensor(out=part, in0=uas[i][:], in1=cs_c[:, :, V_COLS:512], op=ALU.mult)
            gparts[i] = part

        def rope_products(i):
            rr = ropep.tile([P, 2, V_COLS], F32, name="rr")
            nc.vector.tensor_tensor(
                out=rr[:],
                in0=accs[i][:, 0:V_COLS].unsqueeze(1).to_broadcast([P, 2, V_COLS]),
                in1=cs_c[:, :, 0:V_COLS],
                op=ALU.mult,
            )
            ropes[i] = rr

        def rope_sum(i):
            z = zpp.tile([P, TOK_TILES, P], F32, name="z")
            for a in range(TOK_TILES):
                if P * a < V_COLS:
                    both = ropes[i][:, :, P * a : P * (a + 1)]
                else:
                    both = gparts[i][:, :, P * a - V_COLS : P * (a + 1) - V_COLS]
                nc.tensor.matmul(
                    z[:, a, :], lhsT=both[:, 0, :], rhs=ident[:], is_transpose=True, start=True, stop=False
                )
                nc.tensor.matmul(
                    z[:, a, :], lhsT=both[:, 1, :], rhs=swap[:], is_transpose=True, start=False, stop=True
                )
            zs[i] = z

        def is_qk(i):
            return 0 <= i < N_Q + N_KV

        def norm_squares(i):
            if not is_qk(i):
                return
            junk = statp.tile([P, P], BF16, name="junk")
            ss = statp.tile([P, TOK_TILES], F32, name="ss")
            for a in range(TOK_TILES):
                nc.scalar.activation(
                    out=junk[:], in_=zs[i][:, a, :], func=ACT.Square, accum_out=ss[:, a : a + 1]
                )
            stats[i] = ss

        def norm_rsqrt(i):
            if not is_qk(i):
                return
            rs = statp.tile([P, TOK_TILES], F32, name="rs")
            nc.scalar.activation(
                out=rs[:], in_=stats[i][:], func=ACT.Abs_reciprocal_sqrt, scale=1.0 / P, bias=eps[:]
            )
            stats[i] = rs

        def norm_gain(i):
            if not 0 <= i < N_Q:
                return
            rg = statp.tile([P, TOK_TILES], F32, name="rg")
            nc.scalar.activation(out=rg[:], in_=stats[i][:], func=ACT.Copy, scale=gf[:, i : i + 1])
            stats[i] = rg

        def norm_apply(i):
            if not is_qk(i):
                return
            o = outp.tile([P, TOK_TILES, P], F32, name="o")
            for a in range(TOK_TILES):
                nc.scalar.activation(
                    out=o[:, a, :], in_=zs[i][:, a, :], func=ACT.Copy, scale=stats[i][:, a : a + 1]
                )
            if i < N_Q:
                nc.sync.dma_start(out=q_view[:, :, i, :], in_=o[:])
            else:
                nc.sync.dma_start(out=k_view[:, :, i - N_Q, :], in_=o[:])

        def post_v(i):
            o = outp.tile([P, TOK_TILES, P], F32, name="o")
            nc.scalar.copy(out=o[:].rearrange("p a d -> p (a d)"), in_=accs[i][:])
            nc.sync.dma_start(out=v_view[:, :, i - N_Q - N_KV, :], in_=o[:])

        n_qk = N_Q + N_KV
        for s in range(N_W + LAG_S + 1):
            if s < N_W:
                widen(s)
            if s < 2:
                for a in (2 * s, 2 * s + 1):
                    transposes("x%d" % a, xs[a])
            if s == 2:
                table_transposes()
                nc.scalar.copy(out=gf[:], in_=gbf[:])
            if 0 <= s - LAG_T < N_W:
                transposes(s - LAG_T, wide[s - LAG_T])
            matmuls(s - LAG_M, 0)
            if 0 <= s - LAG_P < n_qk:
                rope_sum(s - LAG_P)
            matmuls(s - LAG_M, 1)
            if s < 2:
                for a in (2 * s, 2 * s + 1):
                    evacuate_x(a)
            norm_rsqrt(s - LAG_S)
            evacuate_w(s - LAG_T, 0)
            norm_gain(s - LAG_S)
            evacuate_w(s - LAG_T, 1)
            norm_apply(s - LAG_S)
            norm_squares(s - LAG_P)
            rope_copy(s - LAG_M)
            if n_qk <= s - LAG_M < N_W:
                post_v(s - LAG_M)
            if s == 2:
                for g in range(PASSES):
                    quantise_x(g)
            if 0 <= s - LAG_Q < N_W:
                quantise_w(s - LAG_Q)
            if 0 <= s - LAG_R < n_qk:
                rope_gpsimd(s - LAG_R, s - LAG_Q)
                rope_products(s - LAG_R)
